import numpy as np
import ml_dtypes


def mxq(x, axis, fmt="e4m3"):
    dtype, down = {"e4m3": (ml_dtypes.float8_e4m3fn, 7), "e5m2": (ml_dtypes.float8_e5m2, 14)}[fmt]
    v = np.moveaxis(np.asarray(x, np.float32).astype(ml_dtypes.bfloat16).astype(np.float64), axis, -1)
    blocks = v.reshape(v.shape[:-1] + (-1, 32))
    amax = np.abs(blocks).max(-1, keepdims=True)
    byte = np.maximum(np.where(amax > 0, np.frexp(amax)[1] - 1 + 127, 0) - down, 1)
    scale = np.exp2(byte - 127.0)
    codes = (blocks / scale).astype(np.float32).astype(dtype).astype(np.float64)
    return np.moveaxis((codes * scale).reshape(v.shape), -1, axis)


WIDE = False


def mx_kscale(k):
    if not WIDE:
        return np.ones(k)
    levels = np.array([10, -10, 5, -5, 0])
    a = np.random.permutation(np.resize(levels, k // 512 * 4)).reshape(k // 512, 4)
    idx = np.arange(k)
    return np.exp2(a[idx // 512, idx % 128 // 32])


BF16 = ml_dtypes.bfloat16


def bf(x):
    return np.asarray(x, np.float32).astype(BF16)


def f64(x):
    return np.asarray(x).astype(np.float64)


B, T, DM, DH, L = 4, 2048, 512, 256, 512


def setup_inputs():
    s, u = mx_kscale(DM), mx_kscale(DM)
    return {"k": bf(np.random.standard_normal((B, T, DM)) * s),
            "v": bf(np.random.standard_normal((B, T, DM)) * u),
            "Wk": bf(np.random.standard_normal((DH, DM)) / np.sqrt(DM) / s),
            "Wv": bf(np.random.standard_normal((DH, DM)) * 3.0 / np.sqrt(DM) / u)}


def reference(k, v, Wk, Wv):
    K = mxq(f64(k), 2, "e4m3") @ mxq(f64(Wk), 1, "e4m3").T
    V = mxq(f64(v), 2, "e4m3") @ mxq(f64(Wv), 1, "e4m3").T
    max_key = K.max(axis=0, keepdims=True)
    exp_key = np.exp(K - max_key)
    return exp_key * V, exp_key

@@ -1,0 +1,179 @@
+from contextlib import ExitStack
+
+import concourse.mybir as mybir
+from concourse.masks import make_identity
+
+F32 = mybir.dt.float32
+BF16 = mybir.dt.bfloat16
+U32 = mybir.dt.uint32
+U8 = mybir.dt.uint8
+FP8X4 = mybir.dt.float8_e4m3fn_x4
+
+P = 128
+PACK = 4
+B, T, DM, DH = 4, 2048, 512, 256
+WORDS = DM // 2
+HALVES = DH // P
+STEPS = T // P
+J_LOAD = 2
+J_STORE = 2
+LOAD_BUFS = 6
+CHUNKS = STEPS // J_LOAD
+
+FLOPS = 2 * 2 * B * T * DM * DH
+
+
+def tile_aftfull_pa_t_kernel(tc, k, v, Wk, Wv, out_0, out_1):
+    nc = tc.nc
+    with ExitStack() as ctx:
+        consts = ctx.enter_context(tc.tile_pool(name="consts", bufs=1))
+        loads = ctx.enter_context(tc.tile_pool(name="loads", bufs=LOAD_BUFS))
+        stage = ctx.enter_context(tc.tile_pool(name="stage", bufs=2))
+        maxima = ctx.enter_context(tc.tile_pool(name="maxima", bufs=2 * HALVES))
+        results = ctx.enter_context(tc.tile_pool(name="results", bufs=3))
+        psum_t = ctx.enter_context(tc.psum_pool(name="psum_t", bufs=4))
+        psum_k = ctx.enter_context(tc.psum_pool(name="psum_k", bufs=HALVES))
+        psum_v = ctx.enter_context(tc.psum_pool(name="psum_v", bufs=HALVES))
+        ctx.enter_context(tc.manual_schedule())
+
+        k_rows = k.rearrange("b (p j) d -> p b j d", j=STEPS)
+        v_rows = v.rearrange("b (p j) d -> p b j d", j=STEPS)
+        ev_rows = out_0.rearrange("b (p j) c -> p b j c", j=STEPS)
+        e_rows = out_1.rearrange("b (p j) c -> p b j c", j=STEPS)
+
+        k_chunks = {}
+        v_chunks = {}
+
+        def fetch(c):
+            steps = slice(c * J_LOAD, (c + 1) * J_LOAD)
+            k_chunk = loads.tile([P, B, J_LOAD, DM], BF16)
+            nc.sync.dma_start(out=k_chunk[:], in_=k_rows[:, :, steps, :])
+            v_chunk = loads.tile([P, B, J_LOAD, DM], BF16)
+            nc.sync.dma_start(out=v_chunk[:], in_=v_rows[:, :, steps, :])
+            k_chunks[c] = k_chunk
+            v_chunks[c] = v_chunk
+
+        def refill_after(g):
+            if g % J_LOAD == J_LOAD - 1 and g // J_LOAD + LOAD_BUFS < CHUNKS:
+                fetch(g // J_LOAD + LOAD_BUFS)
+
+        def rows_of_step(chunks, g):
+            words = chunks[g // J_LOAD][:].bitcast(F32)
+            return [words[:, b, g % J_LOAD, :] for b in range(B)]
+
+        def transpose_rows(rows):
+            banks = []
+            for pair in range(2):
+                xt = psum_t.tile([P, 2, 2, P], F32)
+                for i in range(2):
+                    for u in range(2):
+                        nc.tensor.transpose(xt[:, i, u, :], rows[2 * pair + i][:, u * P : (u + 1) * P], identity[:])
+                banks.append(xt)
+            return banks
+
+        def regroup(banks, which):
+            grouped = stage.tile([P, B, P, PACK], BF16, tag="grouped_" + which, align_bytes=64)
+            words = grouped[:].bitcast(F32)
+            for pair in range(2):
+                nc.scalar.copy(out=words[:, 2 * pair : 2 * pair + 2, :, :], in_=banks[pair][:].rearrange("p i u r -> p i r u"))
+            return grouped
+
+        def quantise(pool, grouped, which):
+            codes = pool.tile([P, B * P], U32, tag="codes_" + which, align_bytes=64)
+            scales = pool.tile([P, B * P], U8, tag="scales_" + which, align_bytes=64)
+            nc.vector.quantize_mx(
+                out=codes[:].bitcast(FP8X4), scales=scales[:], in_=grouped[:].rearrange("p b r t -> p (b r t)")
+            )
+            return codes, scales
+
+        def project(pool, operand, first_w_block):
+            codes, scales = operand
+            accs = []
+            for h in range(HALVES):
+                acc = pool.tile([P, B, P], F32)
+                w_cols = slice((first_w_block + h) * P, (first_w_block + h + 1) * P)
+                for b in range(B):
+                    tokens = slice(b * P, (b + 1) * P)
+                    nc.tensor.matmul_mx(
+                        out=acc[:, b, :],
+                        lhsT=codes[:, tokens].bitcast(FP8X4),
+                        lhsT_scale=scales[:, tokens],
+                        rhs=w_codes[:, w_cols].bitcast(FP8X4),
+                        rhs_scale=w_scales[:, w_cols],
+                        start=True,
+                        stop=True,
+                    )
+                accs.append(acc)
+            return accs
+
+        identity = consts.tile([P, P], F32)
+        make_identity(nc, identity[:])
+        warm = consts.tile([P, 1], F32)
+        nc.vector.memset(warm[:], 0.0)
+        nc.scalar.activation(out=warm[:], in_=warm[:], func=mybir.ActivationFunctionType.Exp)
+
+        w_raw = consts.tile([P, 2 * HALVES, DM], BF16)
+        nc.sync.dma_start(out=w_raw[:, 0:HALVES, :], in_=Wk.rearrange("(i p) d -> p i d", p=P))
+        nc.sync.dma_start(out=w_raw[:, HALVES : 2 * HALVES, :], in_=Wv.rearrange("(i p) d -> p i d", p=P))
+        for c in range(LOAD_BUFS):
+            fetch(c)
+
+        w_words = w_raw[:].bitcast(F32)
+        w_grouped = regroup(transpose_rows([w_words[:, i, :] for i in range(2 * HALVES)]), "w")
+        w_codes, w_scales = quantise(consts, w_grouped, "w")
+
+        k_grouped = {}
+        v_grouped = {}
+        k_grouped[0] = regroup(transpose_rows(rows_of_step(k_chunks, 0)), "k")
+        k_acc = project(psum_k, quantise(stage, k_grouped[0], "k"), 0)
+        k_grouped[1] = regroup(transpose_rows(rows_of_step(k_chunks, 1)), "k")
+        v_grouped[0] = regroup(transpose_rows(rows_of_step(v_chunks, 0)), "v")
+        v_grouped[1] = regroup(transpose_rows(rows_of_step(v_chunks, 1)), "v")
+        refill_after(0)
+        refill_after(1)
+
+        for g in range(STEPS):
+            ahead = g + 2
+            jj = g % J_STORE
+            store_steps = slice(g - jj, g - jj + J_STORE)
+            if jj == 0:
+                e_tile = results.tile([P, B, J_STORE, DH], F32)
+                ev_tile = results.tile([P, B, J_STORE, DH], F32)
+
+            if ahead < STEPS:
+                k_grouped[ahead] = regroup(transpose_rows(rows_of_step(k_chunks, ahead)), "k")
+                v_banks = transpose_rows(rows_of_step(v_chunks, ahead))
+                refill_after(ahead)
+
+            tops = []
+            for h in range(HALVES):
+                top = maxima.tile([P, P], F32)
+                nc.vector.tensor_reduce(
+                    out=top[:], in_=k_acc[h][:].rearrange("p b c -> p c b"), axis=mybir.AxisListType.X, op=mybir.AluOpType.max
+                )
+                tops.append(top)
+
+            v_acc = project(psum_v, quantise(stage, v_grouped[g], "v"), HALVES)
+
+            for h in range(HALVES):
+                e_half = e_tile[:, :, jj, h * P : (h + 1) * P]
+                nc.vector.tensor_tensor(
+                    out=e_half, in0=k_acc[h][:], in1=tops[h][:].unsqueeze(1).to_broadcast([P, B, P]), op=mybir.AluOpType.subtract
+                )
+                nc.scalar.activation(out=e_half, in_=e_half, func=mybir.ActivationFunctionType.Exp)
+            if jj == J_STORE - 1:
+                nc.sync.dma_start(out=e_rows[:, :, store_steps, :], in_=e_tile[:])
+
+            if ahead < STEPS:
+                v_grouped[ahead] = regroup(v_banks, "v")
+
+            if g + 1 < STEPS:
+                k_acc = project(psum_k, quantise(stage, k_grouped[g + 1], "k"), 0)
+
+            for h in range(HALVES):
+                cols = slice(h * P, (h + 1) * P)
+                nc.vector.tensor_tensor(
+                    out=ev_tile[:, :, jj, cols], in0=v_acc[h][:], in1=e_tile[:, :, jj, cols], op=mybir.AluOpType.mult
+                )
+            if jj == J_STORE - 1:
+                nc.sync.dma_start(out=ev_rows[:, :, store_steps, :], in_=ev_tile[:])

@@ -126,8 +126,9 @@ def tile_aftfull_pa_t_kernel(tc, k, v, Wk, Wv, out_0, out_1):
         v_grouped = {}
         k_grouped[0] = regroup(transpose_rows(rows_of_step(k_chunks, 0)), "k")
         k_acc = project(psum_k, quantise(stage, k_grouped[0], "k"), 0)
-        k_grouped[1] = regroup(transpose_rows(rows_of_step(k_chunks, 1)), "k")
         v_grouped[0] = regroup(transpose_rows(rows_of_step(v_chunks, 0)), "v")
+        v_acc = project(psum_v, quantise(stage, v_grouped[0], "v"), HALVES)
+        k_grouped[1] = regroup(transpose_rows(rows_of_step(k_chunks, 1)), "k")
         v_grouped[1] = regroup(transpose_rows(rows_of_step(v_chunks, 1)), "v")
         refill_after(0)
         refill_after(1)
@@ -152,9 +153,6 @@ def tile_aftfull_pa_t_kernel(tc, k, v, Wk, Wv, out_0, out_1):
                     out=top[:], in_=k_acc[h][:].rearrange("p b c -> p c b"), axis=mybir.AxisListType.X, op=mybir.AluOpType.max
                 )
                 tops.append(top)
-
-            v_acc = project(psum_v, quantise(stage, v_grouped[g], "v"), HALVES)
-
             for h in range(HALVES):
                 e_half = e_tile[:, :, jj, h * P : (h + 1) * P]
                 nc.vector.tensor_tensor(
@@ -164,16 +162,21 @@ def tile_aftfull_pa_t_kernel(tc, k, v, Wk, Wv, out_0, out_1):
             if jj == J_STORE - 1:
                 nc.sync.dma_start(out=e_rows[:, :, store_steps, :], in_=e_tile[:])
 
-            if ahead < STEPS:
-                v_grouped[ahead] = regroup(v_banks, "v")
-
             if g + 1 < STEPS:
                 k_acc = project(psum_k, quantise(stage, k_grouped[g + 1], "k"), 0)
+                v_operand = quantise(stage, v_grouped[g + 1], "v")
 
-            for h in range(HALVES):
-                cols = slice(h * P, (h + 1) * P)
-                nc.vector.tensor_tensor(
-                    out=ev_tile[:, :, jj, cols], in0=v_acc[h][:], in1=e_tile[:, :, jj, cols], op=mybir.AluOpType.mult
-                )
+            v_half = stage.tile([P, B, P], F32)
+            nc.scalar.copy(out=v_half[:], in_=v_acc[1][:])
+            nc.gpsimd.tensor_tensor(
+                out=ev_tile[:, :, jj, P : 2 * P], in0=v_half[:], in1=e_tile[:, :, jj, P : 2 * P], op=mybir.AluOpType.mult
+            )
+            if ahead < STEPS:
+                v_grouped[ahead] = regroup(v_banks, "v")
+            nc.vector.tensor_tensor(
+                out=ev_tile[:, :, jj, 0:P], in0=v_acc[0][:], in1=e_tile[:, :, jj, 0:P], op=mybir.AluOpType.mult
+            )
+            if g + 1 < STEPS:
+                v_acc = project(psum_v, v_operand, HALVES)
             if jj == J_STORE - 1:
                 nc.sync.dma_start(out=ev_rows[:, :, store_steps, :], in_=ev_tile[:])

@@ -17,7 +17,8 @@ HALVES = DH // P
 STEPS = T // P
 J_LOAD = 2
 J_STORE = 2
-LOAD_BUFS = 6
+LOAD_BUFS = 4
+STORE_BUFS = 5
 CHUNKS = STEPS // J_LOAD
 
 FLOPS = 2 * 2 * B * T * DM * DH
@@ -30,7 +31,7 @@ def tile_aftfull_pa_t_kernel(tc, k, v, Wk, Wv, out_0, out_1):
         loads = ctx.enter_context(tc.tile_pool(name="loads", bufs=LOAD_BUFS))
         stage = ctx.enter_context(tc.tile_pool(name="stage", bufs=2))
         maxima = ctx.enter_context(tc.tile_pool(name="maxima", bufs=2 * HALVES))
-        results = ctx.enter_context(tc.tile_pool(name="results", bufs=3))
+        results = ctx.enter_context(tc.tile_pool(name="results", bufs=STORE_BUFS))
         psum_t = ctx.enter_context(tc.psum_pool(name="psum_t", bufs=4))
         psum_k = ctx.enter_context(tc.psum_pool(name="psum_k", bufs=HALVES))
         psum_v = ctx.enter_context(tc.psum_pool(name="psum_v", bufs=HALVES))

@@ -20,6 +20,7 @@ J_STORE = 2
 LOAD_BUFS = 4
 STORE_BUFS = 5
 CHUNKS = STEPS // J_LOAD
+HEAD_CHUNKS = 2
 
 FLOPS = 2 * 2 * B * T * DM * DH
 
@@ -46,11 +47,14 @@ def tile_aftfull_pa_t_kernel(tc, k, v, Wk, Wv, out_0, out_1):
         v_chunks = {}
 
         def fetch(c):
-            steps = slice(c * J_LOAD, (c + 1) * J_LOAD)
             k_chunk = loads.tile([P, B, J_LOAD, DM], BF16)
-            nc.sync.dma_start(out=k_chunk[:], in_=k_rows[:, :, steps, :])
             v_chunk = loads.tile([P, B, J_LOAD, DM], BF16)
-            nc.sync.dma_start(out=v_chunk[:], in_=v_rows[:, :, steps, :])
+            piece = 1 if c < HEAD_CHUNKS else J_LOAD
+            for first in range(0, J_LOAD, piece):
+                inside = slice(first, first + piece)
+                steps = slice(c * J_LOAD + first, c * J_LOAD + first + piece)
+                nc.sync.dma_start(out=k_chunk[:, :, inside, :], in_=k_rows[:, :, steps, :])
+                nc.sync.dma_start(out=v_chunk[:, :, inside, :], in_=v_rows[:, :, steps, :])
             k_chunks[c] = k_chunk
             v_chunks[c] = v_chunk
 
@@ -126,9 +130,9 @@ def tile_aftfull_pa_t_kernel(tc, k, v, Wk, Wv, out_0, out_1):
         k_grouped = {}
         v_grouped = {}
         k_grouped[0] = regroup(transpose_rows(rows_of_step(k_chunks, 0)), "k")
-        k_acc = project(psum_k, quantise(stage, k_grouped[0], "k"), 0)
         v_grouped[0] = regroup(transpose_rows(rows_of_step(v_chunks, 0)), "v")
-        v_acc = project(psum_v, quantise(stage, v_grouped[0], "v"), HALVES)
+        k_acc = project(psum_k, quantise(stage, k_grouped[0], "k"), 0)
+        v_operand = quantise(stage, v_grouped[0], "v")
         k_grouped[1] = regroup(transpose_rows(rows_of_step(k_chunks, 1)), "k")
         v_grouped[1] = regroup(transpose_rows(rows_of_step(v_chunks, 1)), "v")
         refill_after(0)
@@ -146,6 +150,7 @@ def tile_aftfull_pa_t_kernel(tc, k, v, Wk, Wv, out_0, out_1):
                 k_grouped[ahead] = regroup(transpose_rows(rows_of_step(k_chunks, ahead)), "k")
                 v_banks = transpose_rows(rows_of_step(v_chunks, ahead))
                 refill_after(ahead)
+            v_acc = project(psum_v, v_operand, HALVES)
 
             tops = []
             for h in range(HALVES):
@@ -177,7 +182,5 @@ def tile_aftfull_pa_t_kernel(tc, k, v, Wk, Wv, out_0, out_1):
             nc.vector.tensor_tensor(
                 out=ev_tile[:, :, jj, 0:P], in0=v_acc[0][:], in1=e_tile[:, :, jj, 0:P], op=mybir.AluOpType.mult
             )
-            if g + 1 < STEPS:
-                v_acc = project(psum_v, v_operand, HALVES)
             if jj == J_STORE - 1:
                 nc.sync.dma_start(out=ev_rows[:, :, store_steps, :], in_=ev_tile[:])

@@ -16,9 +16,9 @@ WORDS = DM // 2
 HALVES = DH // P
 STEPS = T // P
 J_LOAD = 2
-J_STORE = 2
+J_STORE = 4
 LOAD_BUFS = 4
-STORE_BUFS = 5
+STORE_BUFS = 3
 CHUNKS = STEPS // J_LOAD
 HEAD_CHUNKS = 2
 
@@ -61,6 +61,16 @@ def tile_aftfull_pa_t_kernel(tc, k, v, Wk, Wv, out_0, out_1):
         def refill_after(g):
             if g % J_LOAD == J_LOAD - 1 and g // J_LOAD + LOAD_BUFS < CHUNKS:
                 fetch(g // J_LOAD + LOAD_BUFS)
+
+        def store(rows, result, g):
+            jj = g % J_STORE
+            if g >= STEPS - J_STORE:
+                lo, hi = jj, jj + 1
+            elif jj == J_STORE - 1:
+                lo, hi = 0, J_STORE
+            else:
+                return
+            nc.sync.dma_start(out=rows[:, :, g - jj + lo : g - jj + hi, :], in_=result[:, :, lo:hi, :])
 
         def rows_of_step(chunks, g):
             words = chunks[g // J_LOAD][:].bitcast(F32)
@@ -141,7 +151,6 @@ def tile_aftfull_pa_t_kernel(tc, k, v, Wk, Wv, out_0, out_1):
         for g in range(STEPS):
             ahead = g + 2
             jj = g % J_STORE
-            store_steps = slice(g - jj, g - jj + J_STORE)
             if jj == 0:
                 e_tile = results.tile([P, B, J_STORE, DH], F32)
                 ev_tile = results.tile([P, B, J_STORE, DH], F32)
@@ -165,8 +174,7 @@ def tile_aftfull_pa_t_kernel(tc, k, v, Wk, Wv, out_0, out_1):
                     out=e_half, in0=k_acc[h][:], in1=tops[h][:].unsqueeze(1).to_broadcast([P, B, P]), op=mybir.AluOpType.subtract
                 )
                 nc.scalar.activation(out=e_half, in_=e_half, func=mybir.ActivationFunctionType.Exp)
-            if jj == J_STORE - 1:
-                nc.sync.dma_start(out=e_rows[:, :, store_steps, :], in_=e_tile[:])
+            store(e_rows, e_tile, g)
 
             if g + 1 < STEPS:
                 k_acc = project(psum_k, quantise(stage, k_grouped[g + 1], "k"), 0)
@@ -182,5 +190,4 @@ def tile_aftfull_pa_t_kernel(tc, k, v, Wk, Wv, out_0, out_1):
             nc.vector.tensor_tensor(
                 out=ev_tile[:, :, jj, 0:P], in0=v_acc[0][:], in1=e_tile[:, :, jj, 0:P], op=mybir.AluOpType.mult
             )
-            if jj == J_STORE - 1:
-                nc.sync.dma_start(out=ev_rows[:, :, store_steps, :], in_=ev_tile[:])
+            store(ev_rows, ev_tile, g)

@@ -16,9 +16,9 @@ WORDS = DM // 2
 HALVES = DH // P
 STEPS = T // P
 J_LOAD = 2
-J_STORE = 4
+J_STORE = 2
 LOAD_BUFS = 4
-STORE_BUFS = 3
+STORE_BUFS = 5
 CHUNKS = STEPS // J_LOAD
 HEAD_CHUNKS = 2
 
@@ -61,16 +61,6 @@ def tile_aftfull_pa_t_kernel(tc, k, v, Wk, Wv, out_0, out_1):
         def refill_after(g):
             if g % J_LOAD == J_LOAD - 1 and g // J_LOAD + LOAD_BUFS < CHUNKS:
                 fetch(g // J_LOAD + LOAD_BUFS)
-
-        def store(rows, result, g):
-            jj = g % J_STORE
-            if g >= STEPS - J_STORE:
-                lo, hi = jj, jj + 1
-            elif jj == J_STORE - 1:
-                lo, hi = 0, J_STORE
-            else:
-                return
-            nc.sync.dma_start(out=rows[:, :, g - jj + lo : g - jj + hi, :], in_=result[:, :, lo:hi, :])
 
         def rows_of_step(chunks, g):
             words = chunks[g // J_LOAD][:].bitcast(F32)
@@ -151,6 +141,7 @@ def tile_aftfull_pa_t_kernel(tc, k, v, Wk, Wv, out_0, out_1):
         for g in range(STEPS):
             ahead = g + 2
             jj = g % J_STORE
+            store_steps = slice(g - jj, g - jj + J_STORE)
             if jj == 0:
                 e_tile = results.tile([P, B, J_STORE, DH], F32)
                 ev_tile = results.tile([P, B, J_STORE, DH], F32)
@@ -174,20 +165,19 @@ def tile_aftfull_pa_t_kernel(tc, k, v, Wk, Wv, out_0, out_1):
                     out=e_half, in0=k_acc[h][:], in1=tops[h][:].unsqueeze(1).to_broadcast([P, B, P]), op=mybir.AluOpType.subtract
                 )
                 nc.scalar.activation(out=e_half, in_=e_half, func=mybir.ActivationFunctionType.Exp)
-            store(e_rows, e_tile, g)
+            if jj == J_STORE - 1:
+                nc.sync.dma_start(out=e_rows[:, :, store_steps, :], in_=e_tile[:])
 
             if g + 1 < STEPS:
                 k_acc = project(psum_k, quantise(stage, k_grouped[g + 1], "k"), 0)
                 v_operand = quantise(stage, v_grouped[g + 1], "v")
 
-            v_half = stage.tile([P, B, P], F32)
-            nc.scalar.copy(out=v_half[:], in_=v_acc[1][:])
-            nc.gpsimd.tensor_tensor(
-                out=ev_tile[:, :, jj, P : 2 * P], in0=v_half[:], in1=e_tile[:, :, jj, P : 2 * P], op=mybir.AluOpType.mult
-            )
             if ahead < STEPS:
                 v_grouped[ahead] = regroup(v_banks, "v")
-            nc.vector.tensor_tensor(
-                out=ev_tile[:, :, jj, 0:P], in0=v_acc[0][:], in1=e_tile[:, :, jj, 0:P], op=mybir.AluOpType.mult
-            )
-            store(ev_rows, ev_tile, g)
+            for h in range(HALVES):
+                cols = slice(h * P, (h + 1) * P)
+                nc.vector.tensor_tensor(
+                    out=ev_tile[:, :, jj, cols], in0=v_acc[h][:], in1=e_tile[:, :, jj, cols], op=mybir.AluOpType.mult
+                )
+            if jj == J_STORE - 1:
+                nc.sync.dma_start(out=ev_rows[:, :, store_steps, :], in_=ev_tile[:])

from contextlib import ExitStack

import concourse.mybir as mybir
from concourse.masks import make_identity

F32 = mybir.dt.float32
BF16 = mybir.dt.bfloat16
U32 = mybir.dt.uint32
U8 = mybir.dt.uint8
FP8X4 = mybir.dt.float8_e4m3fn_x4

P = 128
PACK = 4
B, T, DM, DH = 4, 2048, 512, 256
WORDS = DM // 2
HALVES = DH // P
STEPS = T // P
J_LOAD = 2
J_STORE = 2
LOAD_BUFS = 4
STORE_BUFS = 5
CHUNKS = STEPS // J_LOAD
HEAD_CHUNKS = 2

FLOPS = 2 * 2 * B * T * DM * DH


def tile_aftfull_pa_t_kernel(tc, k, v, Wk, Wv, out_0, out_1):
    nc = tc.nc
    with ExitStack() as ctx:
        consts = ctx.enter_context(tc.tile_pool(name="consts", bufs=1))
        loads = ctx.enter_context(tc.tile_pool(name="loads", bufs=LOAD_BUFS))
        stage = ctx.enter_context(tc.tile_pool(name="stage", bufs=2))
        maxima = ctx.enter_context(tc.tile_pool(name="maxima", bufs=2 * HALVES))
        results = ctx.enter_context(tc.tile_pool(name="results", bufs=STORE_BUFS))
        psum_t = ctx.enter_context(tc.psum_pool(name="psum_t", bufs=4))
        psum_k = ctx.enter_context(tc.psum_pool(name="psum_k", bufs=HALVES))
        psum_v = ctx.enter_context(tc.psum_pool(name="psum_v", bufs=HALVES))
        ctx.enter_context(tc.manual_schedule())

        k_rows = k.rearrange("b (p j) d -> p b j d", j=STEPS)
        v_rows = v.rearrange("b (p j) d -> p b j d", j=STEPS)
        ev_rows = out_0.rearrange("b (p j) c -> p b j c", j=STEPS)
        e_rows = out_1.rearrange("b (p j) c -> p b j c", j=STEPS)

        k_chunks = {}
        v_chunks = {}

        def fetch(c):
            k_chunk = loads.tile([P, B, J_LOAD, DM], BF16)
            v_chunk = loads.tile([P, B, J_LOAD, DM], BF16)
            piece = 1 if c < HEAD_CHUNKS else J_LOAD
            for first in range(0, J_LOAD, piece):
                inside = slice(first, first + piece)
                steps = slice(c * J_LOAD + first, c * J_LOAD + first + piece)
                nc.sync.dma_start(out=k_chunk[:, :, inside, :], in_=k_rows[:, :, steps, :])
                nc.sync.dma_start(out=v_chunk[:, :, inside, :], in_=v_rows[:, :, steps, :])
            k_chunks[c] = k_chunk
            v_chunks[c] = v_chunk

        def refill_after(g):
            if g % J_LOAD == J_LOAD - 1 and g // J_LOAD + LOAD_BUFS < CHUNKS:
                fetch(g // J_LOAD + LOAD_BUFS)

        def rows_of_step(chunks, g):
            words = chunks[g // J_LOAD][:].bitcast(F32)
            return [words[:, b, g % J_LOAD, :] for b in range(B)]

        def transpose_rows(rows):
            banks = []
            for pair in range(2):
                xt = psum_t.tile([P, 2, 2, P], F32)
                for i in range(2):
                    for u in range(2):
                        nc.tensor.transpose(xt[:, i, u, :], rows[2 * pair + i][:, u * P : (u + 1) * P], identity[:])
                banks.append(xt)
            return banks

        def regroup(banks, which):
            grouped = stage.tile([P, B, P, PACK], BF16, tag="grouped_" + which, align_bytes=64)
            words = grouped[:].bitcast(F32)
            for pair in range(2):
                nc.scalar.copy(out=words[:, 2 * pair : 2 * pair + 2, :, :], in_=banks[pair][:].rearrange("p i u r -> p i r u"))
            return grouped

        def quantise(pool, grouped, which):
            codes = pool.tile([P, B * P], U32, tag="codes_" + which, align_bytes=64)
            scales = pool.tile([P, B * P], U8, tag="scales_" + which, align_bytes=64)
            nc.vector.quantize_mx(
                out=codes[:].bitcast(FP8X4), scales=scales[:], in_=grouped[:].rearrange("p b r t -> p (b r t)")
            )
            return codes, scales

        def project(pool, operand, first_w_block):
            codes, scales = operand
            accs = []
            for h in range(HALVES):
                acc = pool.tile([P, B, P], F32)
                w_cols = slice((first_w_block + h) * P, (first_w_block + h + 1) * P)
                for b in range(B):
                    tokens = slice(b * P, (b + 1) * P)
                    nc.tensor.matmul_mx(
                        out=acc[:, b, :],
                        lhsT=codes[:, tokens].bitcast(FP8X4),
                        lhsT_scale=scales[:, tokens],
                        rhs=w_codes[:, w_cols].bitcast(FP8X4),
                        rhs_scale=w_scales[:, w_cols],
                        start=True,
                        stop=True,
                    )
                accs.append(acc)
            return accs

        identity = consts.tile([P, P], F32)
        make_identity(nc, identity[:])
        warm = consts.tile([P, 1], F32)
        nc.vector.memset(warm[:], 0.0)
        nc.scalar.activation(out=warm[:], in_=warm[:], func=mybir.ActivationFunctionType.Exp)

        w_raw = consts.tile([P, 2 * HALVES, DM], BF16)
        nc.sync.dma_start(out=w_raw[:, 0:HALVES, :], in_=Wk.rearrange("(i p) d -> p i d", p=P))
        nc.sync.dma_start(out=w_raw[:, HALVES : 2 * HALVES, :], in_=Wv.rearrange("(i p) d -> p i d", p=P))
        for c in range(LOAD_BUFS):
            fetch(c)

        w_words = w_raw[:].bitcast(F32)
        w_grouped = regroup(transpose_rows([w_words[:, i, :] for i in range(2 * HALVES)]), "w")
        w_codes, w_scales = quantise(consts, w_grouped, "w")

        k_grouped = {}
        v_grouped = {}
        k_grouped[0] = regroup(transpose_rows(rows_of_step(k_chunks, 0)), "k")
        v_grouped[0] = regroup(transpose_rows(rows_of_step(v_chunks, 0)), "v")
        k_acc = project(psum_k, quantise(stage, k_grouped[0], "k"), 0)
        v_operand = quantise(stage, v_grouped[0], "v")
        k_grouped[1] = regroup(transpose_rows(rows_of_step(k_chunks, 1)), "k")
        v_grouped[1] = regroup(transpose_rows(rows_of_step(v_chunks, 1)), "v")
        refill_after(0)
        refill_after(1)

        for g in range(STEPS):
            ahead = g + 2
            jj = g % J_STORE
            store_steps = slice(g - jj, g - jj + J_STORE)
            if jj == 0:
                e_tile = results.tile([P, B, J_STORE, DH], F32)
                ev_tile = results.tile([P, B, J_STORE, DH], F32)

            if ahead < STEPS:
                k_grouped[ahead] = regroup(transpose_rows(rows_of_step(k_chunks, ahead)), "k")
                v_banks = transpose_rows(rows_of_step(v_chunks, ahead))
                refill_after(ahead)
            v_acc = project(psum_v, v_operand, HALVES)

            tops = []
            for h in range(HALVES):
                top = maxima.tile([P, P], F32)
                nc.vector.tensor_reduce(
                    out=top[:], in_=k_acc[h][:].rearrange("p b c -> p c b"), axis=mybir.AxisListType.X, op=mybir.AluOpType.max
                )
                tops.append(top)
            for h in range(HALVES):
                e_half = e_tile[:, :, jj, h * P : (h + 1) * P]
                nc.vector.tensor_tensor(
                    out=e_half, in0=k_acc[h][:], in1=tops[h][:].unsqueeze(1).to_broadcast([P, B, P]), op=mybir.AluOpType.subtract
                )
                nc.scalar.activation(out=e_half, in_=e_half, func=mybir.ActivationFunctionType.Exp)
            if jj == J_STORE - 1:
                nc.sync.dma_start(out=e_rows[:, :, store_steps, :], in_=e_tile[:])

            if g + 1 < STEPS:
                k_acc = project(psum_k, quantise(stage, k_grouped[g + 1], "k"), 0)
                v_operand = quantise(stage, v_grouped[g + 1], "v")

            if ahead < STEPS:
                v_grouped[ahead] = regroup(v_banks, "v")
            for h in range(HALVES):
                cols = slice(h * P, (h + 1) * P)
                nc.vector.tensor_tensor(
                    out=ev_tile[:, :, jj, cols], in0=v_acc[h][:], in1=e_tile[:, :, jj, cols], op=mybir.AluOpType.mult
                )
            if jj == J_STORE - 1:
                nc.sync.dma_start(out=ev_rows[:, :, store_steps, :], in_=ev_tile[:])
